import numpy as np
import ml_dtypes


def mxq(x, axis, fmt="e4m3"):
    dtype, down = {"e4m3": (ml_dtypes.float8_e4m3fn, 7), "e5m2": (ml_dtypes.float8_e5m2, 14)}[fmt]
    v = np.moveaxis(np.asarray(x, np.float32).astype(ml_dtypes.bfloat16).astype(np.float64), axis, -1)
    blocks = v.reshape(v.shape[:-1] + (-1, 32))
    amax = np.abs(blocks).max(-1, keepdims=True)
    byte = np.maximum(np.where(amax > 0, np.frexp(amax)[1] - 1 + 127, 0) - down, 1)
    scale = np.exp2(byte - 127.0)
    codes = (blocks / scale).astype(np.float32).astype(dtype).astype(np.float64)
    return np.moveaxis((codes * scale).reshape(v.shape), -1, axis)


WIDE = False


def mx_kscale(k):
    if not WIDE:
        return np.ones(k)
    levels = np.array([10, -10, 5, -5, 0])
    a = np.random.permutation(np.resize(levels, k // 512 * 4)).reshape(k // 512, 4)
    idx = np.arange(k)
    return np.exp2(a[idx // 512, idx % 128 // 32])


BF16 = ml_dtypes.bfloat16


def bf(x):
    return np.asarray(x, np.float32).astype(BF16)


def f64(x):
    return np.asarray(x).astype(np.float64)


B, S, D, H, KV, HD = 2, 2048, 1024, 4, 2, 128
HALF = HD // 2
ROPE_BASE = 1.0e4


def rotate_half(t):
    return np.concatenate((-t[..., HALF:], t[..., :HALF]), axis=-1)


def setup_inputs():
    s = mx_kscale(D)
    inv_freq = 1.0 / ROPE_BASE ** (np.arange(HALF) / HALF)
    freqs = np.outer(np.arange(S), inv_freq)
    emb = np.concatenate((freqs, freqs), axis=-1)
    w = 1.0 / np.sqrt(D)
    return {"x": bf(np.random.standard_normal((B, S, D)) * s),
            "cos": bf(np.cos(emb)),
            "sin": bf(np.sin(emb)),
            "Wq": bf(np.random.standard_normal((D, H * HD)) * w / s[:, None]),
            "Wk": bf(np.random.standard_normal((D, KV * HD)) * w / s[:, None]),
            "Wv": bf(np.random.standard_normal((D, KV * HD)) * w / s[:, None])}


def reference(x, cos, sin, Wq, Wk, Wv):
    xq = mxq(f64(x), 2, "e4m3")
    q = (xq @ mxq(f64(Wq), 0, "e4m3")).reshape(B, S, H, HD)
    k = (xq @ mxq(f64(Wk), 0, "e4m3")).reshape(B, S, KV, HD)
    v = (xq @ mxq(f64(Wv), 0, "e4m3")).reshape(B, S, KV, HD)
    c = f64(cos)[None, :, None, :]
    sn = f64(sin)[None, :, None, :]
    q_rot = q * c + rotate_half(q) * sn
    k_rot = k * c + rotate_half(k) * sn
    return q_rot, k_rot, v

@@ -1,0 +1,225 @@
+from contextlib import ExitStack
+
+import concourse.mybir as mybir
+from concourse.masks import make_identity
+
+F32 = mybir.dt.float32
+BF16 = mybir.dt.bfloat16
+U32 = mybir.dt.uint32
+U8 = mybir.dt.uint8
+FP8X4 = mybir.dt.float8_e4m3fn_x4
+MULT = mybir.AluOpType.mult
+ADD = mybir.AluOpType.add
+
+P = 128
+B, S, D = 2, 2048, 1024
+HD = 128
+HALF = HD // 2
+Q_COLS, K_COLS, V_COLS = 512, 256, 256
+QK_COLS = Q_COLS + K_COLS
+N_COLS = QK_COLS + V_COLS
+K_PASS = 512
+PASSES = D // K_PASS
+PACK = 4
+SLOTS = 2
+BLOCK = P * SLOTS
+N_BLOCKS = B * S // BLOCK
+POS_BLOCKS = S // BLOCK
+WORDS = D // 2
+
+FLOPS = 2 * B * S * D * N_COLS
+
+
+def tile_attention_pa_t_kernel(tc, x, cos, sin, Wq, Wk, Wv, out_0, out_1, out_2):
+    nc = tc.nc
+    x_rows = x.rearrange("b s k -> (b s) k")
+    q_rows = out_0.rearrange("b s h d -> (b s) (h d)")
+    k_rows = out_1.rearrange("b s h d -> (b s) (h d)")
+    v_rows = out_2.rearrange("b s h d -> (b s) (h d)")
+
+    with ExitStack() as ctx:
+        keep = ctx.enter_context(tc.tile_pool(name="keep", bufs=1))
+        x_pool = ctx.enter_context(tc.tile_pool(name="x_pool", bufs=N_BLOCKS))
+        quant = ctx.enter_context(tc.tile_pool(name="quant", bufs=3))
+        result = ctx.enter_context(tc.tile_pool(name="result", bufs=4))
+        xt_psum = ctx.enter_context(tc.psum_pool(name="xt_psum", bufs=2))
+        acc_psum = ctx.enter_context(tc.psum_pool(name="acc_psum", bufs=6))
+
+        def load_weight(w, cols, name):
+            raw = keep.tile([P, PASSES * PACK, cols], BF16, name=name)
+            nc.sync.dma_start(
+                out=raw[:].rearrange("p (j e) n -> p j (e n)", e=2),
+                in_=w.rearrange("(j p e) n -> p j (e n)", p=P, e=2),
+            )
+            return raw
+
+        def load_x(i):
+            x_blk = x_pool.tile([P, SLOTS * D], BF16)
+            nc.sync.dma_start(
+                out=x_blk[:],
+                in_=x_rows[i * BLOCK : (i + 1) * BLOCK, :].rearrange("(p s) k -> p (s k)", s=SLOTS),
+            )
+            return x_blk
+
+        def load_table(table, name):
+            sb = keep.tile([P, POS_BLOCKS, SLOTS, HD], BF16, name=name)
+            nc.sync.dma_start(
+                out=sb[:].rearrange("p n s d -> p n (s d)"),
+                in_=table.rearrange("(n p s) d -> p n (s d)", p=P, s=SLOTS),
+            )
+            return sb
+
+        wq_raw = load_weight(Wq, Q_COLS, "wq_raw")
+        x_tiles = [load_x(0)]
+        cos_sb = load_table(cos, "cos_sb")
+        sin_sb = load_table(sin, "sin_sb")
+        wk_raw = load_weight(Wk, K_COLS, "wk_raw")
+        wv_raw = load_weight(Wv, V_COLS, "wv_raw")
+        for i in range(1, N_BLOCKS):
+            x_tiles.append(load_x(i))
+
+        ident = keep.tile([P, P], F32)
+        make_identity(nc, ident[:])
+
+        grouped_of = {}
+        codes_of = {}
+
+        def transpose_block(i):
+            x_words = x_tiles[i][:].bitcast(F32)
+            grouped = quant.tile([P, SLOTS * D], BF16, align_bytes=64)
+            grouped_words = grouped[:].bitcast(F32)
+            for s in range(SLOTS):
+                xt = xt_psum.tile([P, WORDS], F32)
+                for j in range(WORDS // P):
+                    nc.tensor.transpose(
+                        xt[:, j * P : (j + 1) * P],
+                        x_words[:, s * WORDS + j * P : s * WORDS + (j + 1) * P],
+                        ident[:],
+                    )
+                nc.scalar.copy(
+                    out=grouped_words[:, s * WORDS : (s + 1) * WORDS].rearrange(
+                        "p (c r u) -> p c r u", c=PASSES, u=2
+                    ),
+                    in_=xt[:].rearrange("p (c u r) -> p c r u", c=PASSES, u=2),
+                )
+            grouped_of[i] = grouped
+
+        def quantise_block(i):
+            x_codes = quant.tile([P, SLOTS * PASSES * P], U32, align_bytes=64)
+            x_scales = quant.tile([P, SLOTS * PASSES * P], U8, align_bytes=64)
+            nc.vector.quantize_mx(
+                out=x_codes[:].bitcast(FP8X4), scales=x_scales[:], in_=grouped_of[i][:]
+            )
+            codes_of[i] = (x_codes, x_scales)
+
+        transpose_block(0)
+
+        w_grouped = keep.tile([P, PASSES, N_COLS, PACK], BF16, align_bytes=64)
+        w_codes = keep.tile([P, PASSES, N_COLS], U32, align_bytes=64)
+        w_scales = keep.tile([P, PASSES, N_COLS], U8, align_bytes=64)
+
+        def regroup_weight(copy, raw, first, cols):
+            for c in range(PASSES):
+                copy(
+                    out=w_grouped[:, c, first : first + cols, :].rearrange(
+                        "p (n i) t -> p n t i", i=4
+                    ),
+                    in_=raw[:, c * PACK : (c + 1) * PACK, :].rearrange("p t (n i) -> p n t i", i=4),
+                )
+
+        def quantise_weight(first, cols):
+            for c in range(PASSES):
+                nc.vector.quantize_mx(
+                    out=w_codes[:, c, first : first + cols].bitcast(FP8X4),
+                    scales=w_scales[:, c, first : first + cols],
+                    in_=w_grouped[:, c, first : first + cols, :].rearrange("p n t -> p (n t)"),
+                )
+
+        regroup_weight(nc.vector.tensor_copy, wq_raw, 0, Q_COLS)
+        regroup_weight(nc.scalar.copy, wk_raw, Q_COLS, K_COLS)
+        regroup_weight(nc.scalar.copy, wv_raw, QK_COLS, V_COLS)
+        quantise_weight(0, Q_COLS)
+        quantise_block(0)
+        nc.vector.tensor_scalar_mul(
+            out=sin_sb[:, :, :, 0:HALF], in0=sin_sb[:, :, :, 0:HALF], scalar1=-1.0
+        )
+        quantise_weight(Q_COLS, K_COLS + V_COLS)
+
+        banks_of = {}
+
+        def project(bank_cols, i, s, first, cols):
+            x_codes, x_scales = codes_of[i]
+            for c in range(PASSES):
+                tokens = slice((s * PASSES + c) * P, (s * PASSES + c + 1) * P)
+                nc.tensor.matmul_mx(
+                    out=bank_cols,
+                    lhsT=x_codes[:, tokens].bitcast(FP8X4),
+                    lhsT_scale=x_scales[:, tokens],
+                    rhs=w_codes[:, c, first : first + cols].bitcast(FP8X4),
+                    rhs_scale=w_scales[:, c, first : first + cols],
+                    start=(c == 0),
+                    stop=(c == PASSES - 1),
+                )
+
+        def project_block(i):
+            q_banks = []
+            for s in range(SLOTS):
+                q_bank = acc_psum.tile([P, Q_COLS], F32, tag="acc")
+                project(q_bank[:], i, s, 0, Q_COLS)
+                q_banks.append(q_bank)
+            k_bank = acc_psum.tile([P, SLOTS * K_COLS], F32, tag="acc")
+            for s in range(SLOTS):
+                project(k_bank[:, s * K_COLS : (s + 1) * K_COLS], i, s, Q_COLS, K_COLS)
+            v_bank = acc_psum.tile([P, SLOTS * V_COLS], F32, tag="acc")
+            for s in range(SLOTS):
+                project(v_bank[:, s * V_COLS : (s + 1) * V_COLS], i, s, QK_COLS, V_COLS)
+            banks_of[i] = (q_banks, k_bank, v_bank)
+
+        def rope_products(bank, n, first_slot, slots, by_cos_cols, by_sin_cols):
+            heads = bank.shape[1] // (slots * HD)
+            shape = [P, slots, heads, HD]
+            u = bank.rearrange("p (s h d) -> p s h d", s=slots, d=HD)
+            by_cos = by_cos_cols.rearrange("p (s h d) -> p s h d", s=slots, d=HD)
+            by_sin = by_sin_cols.rearrange("p (s h d) -> p s h d", s=slots, d=HD)
+            cos_t = cos_sb[:, n, first_slot : first_slot + slots, :].unsqueeze(2).to_broadcast(shape)
+            sin_t = sin_sb[:, n, first_slot : first_slot + slots, :].unsqueeze(2).to_broadcast(shape)
+            nc.vector.tensor_tensor(out=by_cos, in0=u, in1=cos_t, op=MULT)
+            nc.vector.tensor_tensor(
+                out=by_sin[:, :, :, 0:HALF], in0=u[:, :, :, HALF:HD], in1=sin_t[:, :, :, 0:HALF], op=MULT
+            )
+            nc.vector.tensor_tensor(
+                out=by_sin[:, :, :, HALF:HD], in0=u[:, :, :, 0:HALF], in1=sin_t[:, :, :, HALF:HD], op=MULT
+            )
+
+        def rope_block(i):
+            q_banks, k_bank, v_bank = banks_of[i]
+            n = i % POS_BLOCKS
+            rot = result.tile([P, SLOTS * QK_COLS], F32)
+            by_sin = result.tile([P, SLOTS * QK_COLS], F32)
+            values = result.tile([P, SLOTS * V_COLS], F32)
+            nc.scalar.copy(out=values[:], in_=v_bank[:])
+            for s in range(SLOTS):
+                q_cols = slice(s * Q_COLS, (s + 1) * Q_COLS)
+                rope_products(q_banks[s][:], n, s, 1, rot[:, q_cols], by_sin[:, q_cols])
+            k_cols = slice(SLOTS * Q_COLS, SLOTS * QK_COLS)
+            rope_products(k_bank[:], n, 0, SLOTS, rot[:, k_cols], by_sin[:, k_cols])
+            nc.gpsimd.tensor_tensor(out=rot[:], in0=rot[:], in1=by_sin[:], op=ADD)
+            tokens = slice(i * BLOCK, (i + 1) * BLOCK)
+            nc.sync.dma_start(
+                out=q_rows[tokens, :].rearrange("(p s) c -> p (s c)", s=SLOTS),
+                in_=rot[:, 0 : SLOTS * Q_COLS],
+            )
+            nc.sync.dma_start(
+                out=k_rows[tokens, :].rearrange("(p s) c -> p (s c)", s=SLOTS), in_=rot[:, k_cols]
+            )
+            nc.sync.dma_start(
+                out=v_rows[tokens, :].rearrange("(p s) c -> p (s c)", s=SLOTS), in_=values[:]
+            )
+
+        for i in range(N_BLOCKS):
+            if i + 1 < N_BLOCKS:
+                transpose_block(i + 1)
+            project_block(i)
+            if i + 1 < N_BLOCKS:
+                quantise_block(i + 1)
+            rope_block(i)

@@ -32,10 +32,10 @@ FLOPS = 2 * B * S * D * N_COLS
 
 def tile_attention_pa_t_kernel(tc, x, cos, sin, Wq, Wk, Wv, out_0, out_1, out_2):
     nc = tc.nc
-    x_rows = x.rearrange("b s k -> (b s) k")
-    q_rows = out_0.rearrange("b s h d -> (b s) (h d)")
-    k_rows = out_1.rearrange("b s h d -> (b s) (h d)")
-    v_rows = out_2.rearrange("b s h d -> (b s) (h d)")
+    x_blocks = x.rearrange("b (p n s) k -> b n p (s k)", n=POS_BLOCKS, s=SLOTS)
+    q_blocks = out_0.rearrange("b (p n s) h d -> b n p (s h d)", n=POS_BLOCKS, s=SLOTS)
+    k_blocks = out_1.rearrange("b (p n s) h d -> b n p (s h d)", n=POS_BLOCKS, s=SLOTS)
+    v_blocks = out_2.rearrange("b (p n s) h d -> b n p (s h d)", n=POS_BLOCKS, s=SLOTS)
 
     with ExitStack() as ctx:
         keep = ctx.enter_context(tc.tile_pool(name="keep", bufs=1))
@@ -47,34 +47,32 @@ def tile_attention_pa_t_kernel(tc, x, cos, sin, Wq, Wk, Wv, out_0, out_1, out_2)
 
         def load_weight(w, cols, name):
             raw = keep.tile([P, PASSES * PACK, cols], BF16, name=name)
-            nc.sync.dma_start(
-                out=raw[:].rearrange("p (j e) n -> p j (e n)", e=2),
-                in_=w.rearrange("(j p e) n -> p j (e n)", p=P, e=2),
-            )
+            for c in range(PASSES):
+                nc.sync.dma_start(
+                    out=raw[:, c * PACK : (c + 1) * PACK, :].rearrange("p (u e) n -> p u (e n)", e=2),
+                    in_=w[c * K_PASS : (c + 1) * K_PASS, :].rearrange("(u p e) n -> p u (e n)", p=P, e=2),
+                )
             return raw
 
         def load_x(i):
             x_blk = x_pool.tile([P, SLOTS * D], BF16)
-            nc.sync.dma_start(
-                out=x_blk[:],
-                in_=x_rows[i * BLOCK : (i + 1) * BLOCK, :].rearrange("(p s) k -> p (s k)", s=SLOTS),
-            )
+            nc.sync.dma_start(out=x_blk[:], in_=x_blocks[i // POS_BLOCKS, i % POS_BLOCKS])
             return x_blk
 
         def load_table(table, name):
             sb = keep.tile([P, POS_BLOCKS, SLOTS, HD], BF16, name=name)
             nc.sync.dma_start(
-                out=sb[:].rearrange("p n s d -> p n (s d)"),
-                in_=table.rearrange("(n p s) d -> p n (s d)", p=P, s=SLOTS),
+                out=sb[:].rearrange("p n s d -> p (n s d)"),
+                in_=table.rearrange("(p r) d -> p (r d)", p=P),
             )
             return sb
 
         wq_raw = load_weight(Wq, Q_COLS, "wq_raw")
+        wk_raw = load_weight(Wk, K_COLS, "wk_raw")
+        wv_raw = load_weight(Wv, V_COLS, "wv_raw")
         x_tiles = [load_x(0)]
         cos_sb = load_table(cos, "cos_sb")
         sin_sb = load_table(sin, "sin_sb")
-        wk_raw = load_weight(Wk, K_COLS, "wk_raw")
-        wv_raw = load_weight(Wv, V_COLS, "wv_raw")
         for i in range(1, N_BLOCKS):
             x_tiles.append(load_x(i))
 
@@ -136,14 +134,14 @@ def tile_attention_pa_t_kernel(tc, x, cos, sin, Wq, Wk, Wv, out_0, out_1, out_2)
                 )
 
         regroup_weight(nc.vector.tensor_copy, wq_raw, 0, Q_COLS)
-        regroup_weight(nc.scalar.copy, wk_raw, Q_COLS, K_COLS)
+        regroup_weight(nc.vector.tensor_copy, wk_raw, Q_COLS, K_COLS)
         regroup_weight(nc.scalar.copy, wv_raw, QK_COLS, V_COLS)
         quantise_weight(0, Q_COLS)
+        quantise_weight(Q_COLS, K_COLS + V_COLS)
         quantise_block(0)
         nc.vector.tensor_scalar_mul(
             out=sin_sb[:, :, :, 0:HALF], in0=sin_sb[:, :, :, 0:HALF], scalar1=-1.0
         )
-        quantise_weight(Q_COLS, K_COLS + V_COLS)
 
         banks_of = {}
 
@@ -162,14 +160,14 @@ def tile_attention_pa_t_kernel(tc, x, cos, sin, Wq, Wk, Wv, out_0, out_1, out_2)
                 )
 
         def project_block(i):
+            k_bank = acc_psum.tile([P, SLOTS * K_COLS], F32, tag="acc")
+            for s in range(SLOTS):
+                project(k_bank[:, s * K_COLS : (s + 1) * K_COLS], i, s, Q_COLS, K_COLS)
             q_banks = []
             for s in range(SLOTS):
                 q_bank = acc_psum.tile([P, Q_COLS], F32, tag="acc")
                 project(q_bank[:], i, s, 0, Q_COLS)
                 q_banks.append(q_bank)
-            k_bank = acc_psum.tile([P, SLOTS * K_COLS], F32, tag="acc")
-            for s in range(SLOTS):
-                project(k_bank[:, s * K_COLS : (s + 1) * K_COLS], i, s, Q_COLS, K_COLS)
             v_bank = acc_psum.tile([P, SLOTS * V_COLS], F32, tag="acc")
             for s in range(SLOTS):
                 project(v_bank[:, s * V_COLS : (s + 1) * V_COLS], i, s, QK_COLS, V_COLS)
@@ -198,23 +196,25 @@ def tile_attention_pa_t_kernel(tc, x, cos, sin, Wq, Wk, Wv, out_0, out_1, out_2)
             by_sin = result.tile([P, SLOTS * QK_COLS], F32)
             values = result.tile([P, SLOTS * V_COLS], F32)
             nc.scalar.copy(out=values[:], in_=v_bank[:])
+            all_q = slice(0, SLOTS * Q_COLS)
+            all_k = slice(SLOTS * Q_COLS, SLOTS * QK_COLS)
+            rope_products(k_bank[:], n, 0, SLOTS, rot[:, all_k], by_sin[:, all_k])
             for s in range(SLOTS):
                 q_cols = slice(s * Q_COLS, (s + 1) * Q_COLS)
                 rope_products(q_banks[s][:], n, s, 1, rot[:, q_cols], by_sin[:, q_cols])
-            k_cols = slice(SLOTS * Q_COLS, SLOTS * QK_COLS)
-            rope_products(k_bank[:], n, 0, SLOTS, rot[:, k_cols], by_sin[:, k_cols])
-            nc.gpsimd.tensor_tensor(out=rot[:], in0=rot[:], in1=by_sin[:], op=ADD)
-            tokens = slice(i * BLOCK, (i + 1) * BLOCK)
-            nc.sync.dma_start(
-                out=q_rows[tokens, :].rearrange("(p s) c -> p (s c)", s=SLOTS),
-                in_=rot[:, 0 : SLOTS * Q_COLS],
-            )
-            nc.sync.dma_start(
-                out=k_rows[tokens, :].rearrange("(p s) c -> p (s c)", s=SLOTS), in_=rot[:, k_cols]
-            )
-            nc.sync.dma_start(
-                out=v_rows[tokens, :].rearrange("(p s) c -> p (s c)", s=SLOTS), in_=values[:]
-            )
+            if i + 1 < N_BLOCKS:
+                nc.gpsimd.tensor_tensor(out=rot[:], in0=rot[:], in1=by_sin[:], op=ADD)
+            else:
+                nc.gpsimd.tensor_tensor(
+                    out=rot[:, all_k], in0=rot[:, all_k], in1=by_sin[:, all_k], op=ADD
+                )
+                nc.vector.tensor_tensor(
+                    out=rot[:, all_q], in0=rot[:, all_q], in1=by_sin[:, all_q], op=ADD
+                )
+            b = i // POS_BLOCKS
+            nc.sync.dma_start(out=v_blocks[b, n], in_=values[:])
+            nc.sync.dma_start(out=k_blocks[b, n], in_=rot[:, all_k])
+            nc.sync.dma_start(out=q_blocks[b, n], in_=rot[:, all_q])
 
         for i in range(N_BLOCKS):
             if i + 1 < N_BLOCKS:

@@ -41,7 +41,8 @@ def tile_attention_pa_t_kernel(tc, x, cos, sin, Wq, Wk, Wv, out_0, out_1, out_2)
         keep = ctx.enter_context(tc.tile_pool(name="keep", bufs=1))
         x_pool = ctx.enter_context(tc.tile_pool(name="x_pool", bufs=N_BLOCKS))
         quant = ctx.enter_context(tc.tile_pool(name="quant", bufs=3))
-        result = ctx.enter_context(tc.tile_pool(name="result", bufs=4))
+        product = ctx.enter_context(tc.tile_pool(name="product", bufs=3))
+        result = ctx.enter_context(tc.tile_pool(name="result", bufs=7))
         xt_psum = ctx.enter_context(tc.psum_pool(name="xt_psum", bufs=2))
         acc_psum = ctx.enter_context(tc.psum_pool(name="acc_psum", bufs=6))
 
@@ -193,7 +194,7 @@ def tile_attention_pa_t_kernel(tc, x, cos, sin, Wq, Wk, Wv, out_0, out_1, out_2)
             q_banks, k_bank, v_bank = banks_of[i]
             n = i % POS_BLOCKS
             rot = result.tile([P, SLOTS * QK_COLS], F32)
-            by_sin = result.tile([P, SLOTS * QK_COLS], F32)
+            by_sin = product.tile([P, SLOTS * QK_COLS], F32)
             values = result.tile([P, SLOTS * V_COLS], F32)
             nc.scalar.copy(out=values[:], in_=v_bank[:])
             all_q = slice(0, SLOTS * Q_COLS)

@@ -26,6 +26,7 @@ BLOCK = P * SLOTS
 N_BLOCKS = B * S // BLOCK
 POS_BLOCKS = S // BLOCK
 WORDS = D // 2
+VECTOR_ADD_COLS = HD
 
 FLOPS = 2 * B * S * D * N_COLS
 
@@ -41,8 +42,7 @@ def tile_attention_pa_t_kernel(tc, x, cos, sin, Wq, Wk, Wv, out_0, out_1, out_2)
         keep = ctx.enter_context(tc.tile_pool(name="keep", bufs=1))
         x_pool = ctx.enter_context(tc.tile_pool(name="x_pool", bufs=N_BLOCKS))
         quant = ctx.enter_context(tc.tile_pool(name="quant", bufs=3))
-        product = ctx.enter_context(tc.tile_pool(name="product", bufs=3))
-        result = ctx.enter_context(tc.tile_pool(name="result", bufs=7))
+        result = ctx.enter_context(tc.tile_pool(name="result", bufs=6))
         xt_psum = ctx.enter_context(tc.psum_pool(name="xt_psum", bufs=2))
         acc_psum = ctx.enter_context(tc.psum_pool(name="acc_psum", bufs=6))
 
@@ -60,21 +60,20 @@ def tile_attention_pa_t_kernel(tc, x, cos, sin, Wq, Wk, Wv, out_0, out_1, out_2)
             nc.sync.dma_start(out=x_blk[:], in_=x_blocks[i // POS_BLOCKS, i % POS_BLOCKS])
             return x_blk
 
-        def load_table(table, name):
-            sb = keep.tile([P, POS_BLOCKS, SLOTS, HD], BF16, name=name)
-            nc.sync.dma_start(
-                out=sb[:].rearrange("p n s d -> p (n s d)"),
-                in_=table.rearrange("(p r) d -> p (r d)", p=P),
-            )
-            return sb
-
         wq_raw = load_weight(Wq, Q_COLS, "wq_raw")
         wk_raw = load_weight(Wk, K_COLS, "wk_raw")
         wv_raw = load_weight(Wv, V_COLS, "wv_raw")
-        x_tiles = [load_x(0)]
-        cos_sb = load_table(cos, "cos_sb")
-        sin_sb = load_table(sin, "sin_sb")
-        for i in range(1, N_BLOCKS):
+        x_tiles = [load_x(0), load_x(1)]
+        sin_raw = keep.tile([P, POS_BLOCKS, SLOTS, HD], BF16)
+        nc.sync.dma_start(
+            out=sin_raw[:].rearrange("p n s d -> p (n s d)"), in_=sin.rearrange("(p r) d -> p (r d)", p=P)
+        )
+        tables = keep.tile([P, POS_BLOCKS, 2, SLOTS, HD], BF16)
+        nc.sync.dma_start(
+            out=tables[:, :, 0, :, :].rearrange("p n s d -> p n (s d)"),
+            in_=cos.rearrange("(p n s) d -> p n (s d)", p=P, s=SLOTS),
+        )
+        for i in range(2, N_BLOCKS):
             x_tiles.append(load_x(i))
 
         ident = keep.tile([P, P], F32)
@@ -140,8 +139,9 @@ def tile_attention_pa_t_kernel(tc, x, cos, sin, Wq, Wk, Wv, out_0, out_1, out_2)
         quantise_weight(0, Q_COLS)
         quantise_weight(Q_COLS, K_COLS + V_COLS)
         quantise_block(0)
+        nc.vector.tensor_copy(out=tables[:, :, 1, :, 0:HALF], in_=sin_raw[:, :, :, HALF:HD])
         nc.vector.tensor_scalar_mul(
-            out=sin_sb[:, :, :, 0:HALF], in0=sin_sb[:, :, :, 0:HALF], scalar1=-1.0
+            out=tables[:, :, 1, :, HALF:HD], in0=sin_raw[:, :, :, 0:HALF], scalar1=-1.0
         )
 
         banks_of = {}
@@ -174,44 +174,39 @@ def tile_attention_pa_t_kernel(tc, x, cos, sin, Wq, Wk, Wv, out_0, out_1, out_2)
                 project(v_bank[:, s * V_COLS : (s + 1) * V_COLS], i, s, QK_COLS, V_COLS)
             banks_of[i] = (q_banks, k_bank, v_bank)
 
-        def rope_products(bank, n, first_slot, slots, by_cos_cols, by_sin_cols):
+        def rope_products(bank, n, first_slot, slots, products):
             heads = bank.shape[1] // (slots * HD)
-            shape = [P, slots, heads, HD]
-            u = bank.rearrange("p (s h d) -> p s h d", s=slots, d=HD)
-            by_cos = by_cos_cols.rearrange("p (s h d) -> p s h d", s=slots, d=HD)
-            by_sin = by_sin_cols.rearrange("p (s h d) -> p s h d", s=slots, d=HD)
-            cos_t = cos_sb[:, n, first_slot : first_slot + slots, :].unsqueeze(2).to_broadcast(shape)
-            sin_t = sin_sb[:, n, first_slot : first_slot + slots, :].unsqueeze(2).to_broadcast(shape)
-            nc.vector.tensor_tensor(out=by_cos, in0=u, in1=cos_t, op=MULT)
+            shape = [P, 2, slots, heads, HD]
             nc.vector.tensor_tensor(
-                out=by_sin[:, :, :, 0:HALF], in0=u[:, :, :, HALF:HD], in1=sin_t[:, :, :, 0:HALF], op=MULT
+                out=products.rearrange("p w (s h d) -> p w s h d", s=slots, d=HD),
+                in0=bank.rearrange("p (s h d) -> p s h d", s=slots, d=HD).unsqueeze(1).to_broadcast(shape),
+                in1=tables[:, n, :, first_slot : first_slot + slots, :].unsqueeze(3).to_broadcast(shape),
+                op=MULT,
             )
-            nc.vector.tensor_tensor(
-                out=by_sin[:, :, :, HALF:HD], in0=u[:, :, :, 0:HALF], in1=sin_t[:, :, :, HALF:HD], op=MULT
-            )
+
+        def add_products(engine, both, cols):
+            by_cos = both[:, 0, cols].rearrange("p (g t j) -> p g t j", t=2, j=HALF)
+            by_sin = both[:, 1, cols].rearrange("p (g t j) -> p g t j", t=2, j=HALF)
+            engine.tensor_tensor(out=by_cos, in0=by_cos, in1=by_sin[:, :, ::-1, :], op=ADD)
 
         def rope_block(i):
             q_banks, k_bank, v_bank = banks_of[i]
             n = i % POS_BLOCKS
-            rot = result.tile([P, SLOTS * QK_COLS], F32)
-            by_sin = product.tile([P, SLOTS * QK_COLS], F32)
+            both = result.tile([P, 2, SLOTS * QK_COLS], F32)
             values = result.tile([P, SLOTS * V_COLS], F32)
             nc.scalar.copy(out=values[:], in_=v_bank[:])
             all_q = slice(0, SLOTS * Q_COLS)
             all_k = slice(SLOTS * Q_COLS, SLOTS * QK_COLS)
-            rope_products(k_bank[:], n, 0, SLOTS, rot[:, all_k], by_sin[:, all_k])
+            rope_products(k_bank[:], n, 0, SLOTS, both[:, :, all_k])
             for s in range(SLOTS):
-                q_cols = slice(s * Q_COLS, (s + 1) * Q_COLS)
-                rope_products(q_banks[s][:], n, s, 1, rot[:, q_cols], by_sin[:, q_cols])
+                rope_products(q_banks[s][:], n, s, 1, both[:, :, s * Q_COLS : (s + 1) * Q_COLS])
             if i + 1 < N_BLOCKS:
-                nc.gpsimd.tensor_tensor(out=rot[:], in0=rot[:], in1=by_sin[:], op=ADD)
+                add_products(nc.vector, both, slice(SLOTS * QK_COLS - VECTOR_ADD_COLS, SLOTS * QK_COLS))
+                add_products(nc.gpsimd, both, slice(0, SLOTS * QK_COLS - VECTOR_ADD_COLS))
             else:
-                nc.gpsimd.tensor_tensor(
-                    out=rot[:, all_k], in0=rot[:, all_k], in1=by_sin[:, all_k], op=ADD
-                )
-                nc.vector.tensor_tensor(
-                    out=rot[:, all_q], in0=rot[:, all_q], in1=by_sin[:, all_q], op=ADD
-                )
+                add_products(nc.gpsimd, both, all_k)
+                add_products(nc.vector, both, all_q)
+            rot = both[:, 0, :]
             b = i // POS_BLOCKS
             nc.sync.dma_start(out=v_blocks[b, n], in_=values[:])
             nc.sync.dma_start(out=k_blocks[b, n], in_=rot[:, all_k])

from contextlib import ExitStack

import concourse.mybir as mybir
from concourse.masks import make_identity

F32 = mybir.dt.float32
BF16 = mybir.dt.bfloat16
U32 = mybir.dt.uint32
U8 = mybir.dt.uint8
FP8X4 = mybir.dt.float8_e4m3fn_x4
MULT = mybir.AluOpType.mult
ADD = mybir.AluOpType.add

P = 128
B, S, D = 2, 2048, 1024
HD = 128
HALF = HD // 2
Q_COLS, K_COLS, V_COLS = 512, 256, 256
QK_COLS = Q_COLS + K_COLS
N_COLS = QK_COLS + V_COLS
K_PASS = 512
PASSES = D // K_PASS
PACK = 4
SLOTS = 2
BLOCK = P * SLOTS
N_BLOCKS = B * S // BLOCK
POS_BLOCKS = S // BLOCK
WORDS = D // 2
VECTOR_ADD_COLS = HD

FLOPS = 2 * B * S * D * N_COLS


def tile_attention_pa_t_kernel(tc, x, cos, sin, Wq, Wk, Wv, out_0, out_1, out_2):
    nc = tc.nc
    x_blocks = x.rearrange("b (p n s) k -> b n p (s k)", n=POS_BLOCKS, s=SLOTS)
    q_blocks = out_0.rearrange("b (p n s) h d -> b n p (s h d)", n=POS_BLOCKS, s=SLOTS)
    k_blocks = out_1.rearrange("b (p n s) h d -> b n p (s h d)", n=POS_BLOCKS, s=SLOTS)
    v_blocks = out_2.rearrange("b (p n s) h d -> b n p (s h d)", n=POS_BLOCKS, s=SLOTS)

    with ExitStack() as ctx:
        keep = ctx.enter_context(tc.tile_pool(name="keep", bufs=1))
        x_pool = ctx.enter_context(tc.tile_pool(name="x_pool", bufs=N_BLOCKS))
        quant = ctx.enter_context(tc.tile_pool(name="quant", bufs=3))
        result = ctx.enter_context(tc.tile_pool(name="result", bufs=6))
        xt_psum = ctx.enter_context(tc.psum_pool(name="xt_psum", bufs=2))
        acc_psum = ctx.enter_context(tc.psum_pool(name="acc_psum", bufs=6))

        def load_weight(w, cols, name):
            raw = keep.tile([P, PASSES * PACK, cols], BF16, name=name)
            for c in range(PASSES):
                nc.sync.dma_start(
                    out=raw[:, c * PACK : (c + 1) * PACK, :].rearrange("p (u e) n -> p u (e n)", e=2),
                    in_=w[c * K_PASS : (c + 1) * K_PASS, :].rearrange("(u p e) n -> p u (e n)", p=P, e=2),
                )
            return raw

        def load_x(i):
            x_blk = x_pool.tile([P, SLOTS * D], BF16)
            nc.sync.dma_start(out=x_blk[:], in_=x_blocks[i // POS_BLOCKS, i % POS_BLOCKS])
            return x_blk

        wq_raw = load_weight(Wq, Q_COLS, "wq_raw")
        wk_raw = load_weight(Wk, K_COLS, "wk_raw")
        wv_raw = load_weight(Wv, V_COLS, "wv_raw")
        x_tiles = [load_x(0), load_x(1)]
        sin_raw = keep.tile([P, POS_BLOCKS, SLOTS, HD], BF16)
        nc.sync.dma_start(
            out=sin_raw[:].rearrange("p n s d -> p (n s d)"), in_=sin.rearrange("(p r) d -> p (r d)", p=P)
        )
        tables = keep.tile([P, POS_BLOCKS, 2, SLOTS, HD], BF16)
        nc.sync.dma_start(
            out=tables[:, :, 0, :, :].rearrange("p n s d -> p n (s d)"),
            in_=cos.rearrange("(p n s) d -> p n (s d)", p=P, s=SLOTS),
        )
        for i in range(2, N_BLOCKS):
            x_tiles.append(load_x(i))

        ident = keep.tile([P, P], F32)
        make_identity(nc, ident[:])

        grouped_of = {}
        codes_of = {}

        def transpose_block(i):
            x_words = x_tiles[i][:].bitcast(F32)
            grouped = quant.tile([P, SLOTS * D], BF16, align_bytes=64)
            grouped_words = grouped[:].bitcast(F32)
            for s in range(SLOTS):
                xt = xt_psum.tile([P, WORDS], F32)
                for j in range(WORDS // P):
                    nc.tensor.transpose(
                        xt[:, j * P : (j + 1) * P],
                        x_words[:, s * WORDS + j * P : s * WORDS + (j + 1) * P],
                        ident[:],
                    )
                nc.scalar.copy(
                    out=grouped_words[:, s * WORDS : (s + 1) * WORDS].rearrange(
                        "p (c r u) -> p c r u", c=PASSES, u=2
                    ),
                    in_=xt[:].rearrange("p (c u r) -> p c r u", c=PASSES, u=2),
                )
            grouped_of[i] = grouped

        def quantise_block(i):
            x_codes = quant.tile([P, SLOTS * PASSES * P], U32, align_bytes=64)
            x_scales = quant.tile([P, SLOTS * PASSES * P], U8, align_bytes=64)
            nc.vector.quantize_mx(
                out=x_codes[:].bitcast(FP8X4), scales=x_scales[:], in_=grouped_of[i][:]
            )
            codes_of[i] = (x_codes, x_scales)

        transpose_block(0)

        w_grouped = keep.tile([P, PASSES, N_COLS, PACK], BF16, align_bytes=64)
        w_codes = keep.tile([P, PASSES, N_COLS], U32, align_bytes=64)
        w_scales = keep.tile([P, PASSES, N_COLS], U8, align_bytes=64)

        def regroup_weight(copy, raw, first, cols):
            for c in range(PASSES):
                copy(
                    out=w_grouped[:, c, first : first + cols, :].rearrange(
                        "p (n i) t -> p n t i", i=4
                    ),
                    in_=raw[:, c * PACK : (c + 1) * PACK, :].rearrange("p t (n i) -> p n t i", i=4),
                )

        def quantise_weight(first, cols):
            for c in range(PASSES):
                nc.vector.quantize_mx(
                    out=w_codes[:, c, first : first + cols].bitcast(FP8X4),
                    scales=w_scales[:, c, first : first + cols],
                    in_=w_grouped[:, c, first : first + cols, :].rearrange("p n t -> p (n t)"),
                )

        regroup_weight(nc.vector.tensor_copy, wq_raw, 0, Q_COLS)
        regroup_weight(nc.vector.tensor_copy, wk_raw, Q_COLS, K_COLS)
        regroup_weight(nc.scalar.copy, wv_raw, QK_COLS, V_COLS)
        quantise_weight(0, Q_COLS)
        quantise_weight(Q_COLS, K_COLS + V_COLS)
        quantise_block(0)
        nc.vector.tensor_copy(out=tables[:, :, 1, :, 0:HALF], in_=sin_raw[:, :, :, HALF:HD])
        nc.vector.tensor_scalar_mul(
            out=tables[:, :, 1, :, HALF:HD], in0=sin_raw[:, :, :, 0:HALF], scalar1=-1.0
        )

        banks_of = {}

        def project(bank_cols, i, s, first, cols):
            x_codes, x_scales = codes_of[i]
            for c in range(PASSES):
                tokens = slice((s * PASSES + c) * P, (s * PASSES + c + 1) * P)
                nc.tensor.matmul_mx(
                    out=bank_cols,
                    lhsT=x_codes[:, tokens].bitcast(FP8X4),
                    lhsT_scale=x_scales[:, tokens],
                    rhs=w_codes[:, c, first : first + cols].bitcast(FP8X4),
                    rhs_scale=w_scales[:, c, first : first + cols],
                    start=(c == 0),
                    stop=(c == PASSES - 1),
                )

        def project_block(i):
            k_bank = acc_psum.tile([P, SLOTS * K_COLS], F32, tag="acc")
            for s in range(SLOTS):
                project(k_bank[:, s * K_COLS : (s + 1) * K_COLS], i, s, Q_COLS, K_COLS)
            q_banks = []
            for s in range(SLOTS):
                q_bank = acc_psum.tile([P, Q_COLS], F32, tag="acc")
                project(q_bank[:], i, s, 0, Q_COLS)
                q_banks.append(q_bank)
            v_bank = acc_psum.tile([P, SLOTS * V_COLS], F32, tag="acc")
            for s in range(SLOTS):
                project(v_bank[:, s * V_COLS : (s + 1) * V_COLS], i, s, QK_COLS, V_COLS)
            banks_of[i] = (q_banks, k_bank, v_bank)

        def rope_products(bank, n, first_slot, slots, products):
            heads = bank.shape[1] // (slots * HD)
            shape = [P, 2, slots, heads, HD]
            nc.vector.tensor_tensor(
                out=products.rearrange("p w (s h d) -> p w s h d", s=slots, d=HD),
                in0=bank.rearrange("p (s h d) -> p s h d", s=slots, d=HD).unsqueeze(1).to_broadcast(shape),
                in1=tables[:, n, :, first_slot : first_slot + slots, :].unsqueeze(3).to_broadcast(shape),
                op=MULT,
            )

        def add_products(engine, both, cols):
            by_cos = both[:, 0, cols].rearrange("p (g t j) -> p g t j", t=2, j=HALF)
            by_sin = both[:, 1, cols].rearrange("p (g t j) -> p g t j", t=2, j=HALF)
            engine.tensor_tensor(out=by_cos, in0=by_cos, in1=by_sin[:, :, ::-1, :], op=ADD)

        def rope_block(i):
            q_banks, k_bank, v_bank = banks_of[i]
            n = i % POS_BLOCKS
            both = result.tile([P, 2, SLOTS * QK_COLS], F32)
            values = result.tile([P, SLOTS * V_COLS], F32)
            nc.scalar.copy(out=values[:], in_=v_bank[:])
            all_q = slice(0, SLOTS * Q_COLS)
            all_k = slice(SLOTS * Q_COLS, SLOTS * QK_COLS)
            rope_products(k_bank[:], n, 0, SLOTS, both[:, :, all_k])
            for s in range(SLOTS):
                rope_products(q_banks[s][:], n, s, 1, both[:, :, s * Q_COLS : (s + 1) * Q_COLS])
            if i + 1 < N_BLOCKS:
                add_products(nc.vector, both, slice(SLOTS * QK_COLS - VECTOR_ADD_COLS, SLOTS * QK_COLS))
                add_products(nc.gpsimd, both, slice(0, SLOTS * QK_COLS - VECTOR_ADD_COLS))
            else:
                add_products(nc.gpsimd, both, all_k)
                add_products(nc.vector, both, all_q)
            rot = both[:, 0, :]
            b = i // POS_BLOCKS
            nc.sync.dma_start(out=v_blocks[b, n], in_=values[:])
            nc.sync.dma_start(out=k_blocks[b, n], in_=rot[:, all_k])
            nc.sync.dma_start(out=q_blocks[b, n], in_=rot[:, all_q])

        for i in range(N_BLOCKS):
            if i + 1 < N_BLOCKS:
                transpose_block(i + 1)
            project_block(i)
            if i + 1 < N_BLOCKS:
                quantise_block(i + 1)
            rope_block(i)
